import numpy as np
import ml_dtypes


def mxq(x, axis, fmt="e4m3"):
    dtype, down = {"e4m3": (ml_dtypes.float8_e4m3fn, 7), "e5m2": (ml_dtypes.float8_e5m2, 14)}[fmt]
    v = np.moveaxis(np.asarray(x, np.float32).astype(ml_dtypes.bfloat16).astype(np.float64), axis, -1)
    blocks = v.reshape(v.shape[:-1] + (-1, 32))
    amax = np.abs(blocks).max(-1, keepdims=True)
    byte = np.maximum(np.where(amax > 0, np.frexp(amax)[1] - 1 + 127, 0) - down, 1)
    scale = np.exp2(byte - 127.0)
    codes = (blocks / scale).astype(np.float32).astype(dtype).astype(np.float64)
    return np.moveaxis((codes * scale).reshape(v.shape), -1, axis)


WIDE = False


def mx_kscale(k):
    if not WIDE:
        return np.ones(k)
    levels = np.array([10, -10, 5, -5, 0])
    a = np.random.permutation(np.resize(levels, k // 512 * 4)).reshape(k // 512, 4)
    idx = np.arange(k)
    return np.exp2(a[idx // 512, idx % 128 // 32])


BF16 = ml_dtypes.bfloat16


def bf(x):
    return np.asarray(x, np.float32).astype(BF16)


def f64(x):
    return np.asarray(x).astype(np.float64)


B, N, D, H, DH, GD = 2, 4096, 512, 2, 128, 128
INNER = H * DH


def silu(v):
    return v / (1.0 + np.exp(-v))


def to_heads(t):
    return t.reshape(B, N, H, DH).transpose(0, 2, 1, 3)


def setup_inputs():
    s = mx_kscale(D)
    theta = (10000.0 ** (-2.0 / INNER * np.arange(INNER)) * (1.0 + 0.1 * np.random.standard_normal(INNER))).reshape(H, 1, DH)
    ang = theta * np.arange(N).reshape(1, N, 1)
    return {"x": bf(np.random.standard_normal((B, N, D)) * s),
            "w_k": bf(np.random.standard_normal((D, INNER)) / np.sqrt(D) / s[:, None]),
            "w_v": bf(np.random.standard_normal((D, INNER)) / np.sqrt(D) / s[:, None]),
            "cos_tab": bf(np.cos(ang)), "sin_tab": bf(np.sin(ang))}


def reference(x, w_k, w_v, cos_tab, sin_tab):
    xq = mxq(f64(x), 2, "e4m3")
    k = to_heads(silu(xq @ mxq(f64(w_k), 0, "e4m3")))
    v = to_heads(silu(xq @ mxq(f64(w_v), 0, "e4m3")))
    c, s = f64(cos_tab)[None], f64(sin_tab)[None]
    k_rot = np.concatenate([k * c, k * s], axis=-1) / np.sqrt(2 * DH)
    return mxq(k_rot, 2, "e4m3").transpose(0, 1, 3, 2) @ mxq(v, 2, "e4m3")

@@ -1,0 +1,238 @@
+from contextlib import ExitStack
+
+import concourse.mybir as mybir
+from concourse.masks import make_identity
+
+F32 = mybir.dt.float32
+BF16 = mybir.dt.bfloat16
+U32 = mybir.dt.uint32
+U8 = mybir.dt.uint8
+FP8X4 = mybir.dt.float8_e4m3fn_x4
+SILU = mybir.ActivationFunctionType.Silu
+MULT = mybir.AluOpType.mult
+
+SEQS, POSITIONS, FEATURES, HEADS, HEAD_DIM = 2, 4096, 512, 2, 128
+P = 128
+PACK = 4
+GROUP = P * PACK
+GROUPS_PER_SEQ = POSITIONS // GROUP
+GROUPS = SEQS * GROUPS_PER_SEQ
+HALVES = 2
+WORD_BLOCKS = FEATURES // 2 // P
+COLUMN_BLOCKS = 2 * HEADS
+W_COLUMNS = COLUMN_BLOCKS * HEAD_DIM
+K_ROT_SCALE = 1.0 / 16.0
+
+FLOPS = 2 * SEQS * POSITIONS * FEATURES * W_COLUMNS + 2 * SEQS * HEADS * POSITIONS * HALVES * HEAD_DIM * HEAD_DIM
+
+
+def tile_linearattention_pa_t_kernel(tc, x, w_k, w_v, cos_tab, sin_tab, out):
+    nc = tc.nc
+    with ExitStack() as ctx:
+        const = ctx.enter_context(tc.tile_pool(name="const", bufs=1))
+        x_pool = ctx.enter_context(tc.tile_pool(name="x_rows", bufs=GROUPS))
+        table_pool = ctx.enter_context(tc.tile_pool(name="tables", bufs=GROUPS_PER_SEQ))
+        seq_pool = ctx.enter_context(tc.tile_pool(name="per_sequence", bufs=SEQS))
+        stream = ctx.enter_context(tc.tile_pool(name="stream", bufs=3))
+        flip_psum = ctx.enter_context(tc.psum_pool(name="flip_psum", bufs=3))
+        proj_psum = ctx.enter_context(tc.psum_pool(name="proj_psum", bufs=COLUMN_BLOCKS))
+        state_psum = ctx.enter_context(tc.psum_pool(name="state_psum", bufs=1))
+        ctx.enter_context(tc.manual_schedule())
+
+        x_rows, tables = {}, {}
+
+        def load_x(i):
+            seq, g = divmod(i, GROUPS_PER_SEQ)
+            rows = x_pool.tile([P, PACK, FEATURES], BF16)
+            positions = x[seq, g * GROUP : (g + 1) * GROUP, :]
+            nc.sync.dma_start(out=rows[:], in_=positions.rearrange("(p t) d -> p t d", t=PACK))
+            x_rows[i] = rows
+
+        def load_weight(w, name):
+            raw = const.tile([P, PACK, HEADS * HEAD_DIM], BF16, name=name)
+            nc.sync.dma_start(
+                out=raw[:].rearrange("q (u e) c -> q u (e c)", e=2),
+                in_=w.rearrange("(u q e) c -> q u (e c)", u=WORD_BLOCKS, e=2),
+            )
+            return raw
+
+        def load_tables(g):
+            both = table_pool.tile([P, HALVES, HEADS, PACK, HEAD_DIM], BF16)
+            for half, table in enumerate((cos_tab, sin_tab)):
+                positions = table[:, g * GROUP : (g + 1) * GROUP, :]
+                nc.sync.dma_start(out=both[:, half], in_=positions.rearrange("h (p t) w -> p h t w", t=PACK))
+            tables[g] = both
+
+        load_x(0)
+        raw_k = load_weight(w_k, "raw_k")
+        raw_v = load_weight(w_v, "raw_v")
+        for g in range(GROUPS_PER_SEQ):
+            load_tables(g)
+            if g + 1 < GROUPS_PER_SEQ:
+                load_x(g + 1)
+        for i in range(GROUPS_PER_SEQ, GROUPS):
+            load_x(i)
+
+        identity = const.tile([P, P], F32)
+        make_identity(nc, identity[:])
+        zero = const.tile([P, 1], F32)
+        unused = const.tile([P, 1], F32)
+        nc.vector.memset(zero[:], 0.0)
+        nc.scalar.activation(out=unused[:], in_=zero[:], func=SILU)
+
+        w_grouped = const.tile([P, W_COLUMNS, PACK], BF16, align_bytes=64)
+        w_codes = const.tile([P, W_COLUMNS], U32, align_bytes=64)
+        w_scales = const.tile([P, W_COLUMNS], U8, align_bytes=64)
+        for first, raw in ((0, raw_k), (HEADS * HEAD_DIM, raw_v)):
+            nc.vector.tensor_copy(
+                out=w_grouped[:, first : first + HEADS * HEAD_DIM, :], in_=raw[:].rearrange("p t c -> p c t")
+            )
+        nc.vector.quantize_mx(
+            out=w_codes[:].bitcast(FP8X4), scales=w_scales[:], in_=w_grouped[:].rearrange("p c t -> p (c t)")
+        )
+
+        flipped, x_grouped, x_codes, x_scales, banks, k_act, v_grouped = {}, {}, {}, {}, {}, {}, {}
+        k_codes, k_scales, v_codes, v_scales, state = {}, {}, {}, {}, {}
+
+        def transpose_x(i):
+            for pair in range(PACK // 2):
+                bank = flip_psum.tile([P, 2, WORD_BLOCKS, P], F32, name="flip_bank")
+                for t in range(2):
+                    words = x_rows[i][:, 2 * pair + t, :].bitcast(F32)
+                    for u in range(WORD_BLOCKS):
+                        nc.tensor.transpose(bank[:, t, u, :], words[:, u * P : (u + 1) * P], identity[:])
+                flipped[(i, pair)] = bank
+
+        def copy_flipped(i):
+            grouped = stream.tile([P, GROUP * PACK], BF16, align_bytes=64, name="x_grouped")
+            words = grouped[:].bitcast(F32).rearrange("q (t m u) -> q t m u", t=PACK, u=WORD_BLOCKS)
+            for pair in range(PACK // 2):
+                nc.scalar.copy(
+                    out=words[:, 2 * pair : 2 * pair + 2],
+                    in_=flipped[(i, pair)][:].rearrange("q t u m -> q t m u"),
+                )
+            x_grouped[i] = grouped
+
+        def quantise_x(i):
+            codes = stream.tile([P, GROUP], U32, align_bytes=64, name="x_codes")
+            scales = stream.tile([P, GROUP], U8, align_bytes=64, name="x_scales")
+            nc.vector.quantize_mx(out=codes[:].bitcast(FP8X4), scales=scales[:], in_=x_grouped[i][:])
+            x_codes[i], x_scales[i] = codes, scales
+
+        def project(i, c):
+            bank = proj_psum.tile([P, PACK, HEAD_DIM], F32, name="proj_bank")
+            columns = slice(c * HEAD_DIM, (c + 1) * HEAD_DIM)
+            for t in range(PACK):
+                rows = slice(t * P, (t + 1) * P)
+                nc.tensor.matmul_mx(
+                    out=bank[:, t, :],
+                    lhsT=x_codes[i][:, rows].bitcast(FP8X4),
+                    lhsT_scale=x_scales[i][:, rows],
+                    rhs=w_codes[:, columns].bitcast(FP8X4),
+                    rhs_scale=w_scales[:, columns],
+                    start=True,
+                    stop=True,
+                )
+            banks[(i, c)] = bank
+
+        def open_group(i):
+            k_tile = stream.tile([P, HEADS, HEAD_DIM, PACK], F32, name="k_act")
+            v_tile = stream.tile([P, HEADS, HEAD_DIM, PACK], BF16, align_bytes=64, name="v_grouped")
+            k_act[i], v_grouped[i] = k_tile, v_tile
+
+        def activate(i, c):
+            is_v, h = divmod(c, HEADS)
+            target = v_grouped[i] if is_v else k_act[i]
+            nc.scalar.activation(out=target[:, h], in_=banks[(i, c)][:].rearrange("p t w -> p w t"), func=SILU)
+
+        def open_sequence(seq):
+            kc = seq_pool.tile([P, GROUPS_PER_SEQ, HALVES * HEADS * HEAD_DIM], U32, align_bytes=64, name="k_codes")
+            ks = seq_pool.tile([P, GROUPS_PER_SEQ, HALVES * HEADS * HEAD_DIM], U8, align_bytes=64, name="k_scales")
+            vc = seq_pool.tile([P, GROUPS_PER_SEQ, HEADS * HEAD_DIM], U32, align_bytes=64, name="v_codes")
+            vs = seq_pool.tile([P, GROUPS_PER_SEQ, HEADS * HEAD_DIM], U8, align_bytes=64, name="v_scales")
+            k_codes[seq], k_scales[seq], v_codes[seq], v_scales[seq] = kc, ks, vc, vs
+
+        def rotate(i):
+            g = i % GROUPS_PER_SEQ
+            k_rot = stream.tile([P, HALVES, HEADS, HEAD_DIM, PACK], BF16, align_bytes=64, name="k_rot")
+            for half in range(HALVES):
+                for h in range(HEADS):
+                    nc.vector.scalar_tensor_tensor(
+                        out=k_rot[:, half, h],
+                        in0=k_act[i][:, h],
+                        scalar=K_ROT_SCALE,
+                        in1=tables[g][:, half, h].rearrange("p t w -> p w t"),
+                        op0=MULT,
+                        op1=MULT,
+                    )
+            return k_rot
+
+        def quantise_v(i):
+            seq, g = divmod(i, GROUPS_PER_SEQ)
+            nc.vector.quantize_mx(
+                out=v_codes[seq][:, g, :].bitcast(FP8X4),
+                scales=v_scales[seq][:, g, :],
+                in_=v_grouped[i][:].rearrange("p h w t -> p (h w t)"),
+            )
+
+        def quantise_k_rot(i, k_rot):
+            seq, g = divmod(i, GROUPS_PER_SEQ)
+            nc.vector.quantize_mx(
+                out=k_codes[seq][:, g, :].bitcast(FP8X4),
+                scales=k_scales[seq][:, g, :],
+                in_=k_rot[:].rearrange("p a h w t -> p (a h w t)"),
+            )
+
+        def add_up_state(seq):
+            bank = state_psum.tile([P, HEADS, HALVES, HEAD_DIM], F32, name="state_bank")
+            for h in range(HEADS):
+                for half in range(HALVES):
+                    e_columns = slice((half * HEADS + h) * HEAD_DIM, (half * HEADS + h + 1) * HEAD_DIM)
+                    d_columns = slice(h * HEAD_DIM, (h + 1) * HEAD_DIM)
+                    for g in range(GROUPS_PER_SEQ):
+                        nc.tensor.matmul_mx(
+                            out=bank[:, h, half, :],
+                            lhsT=k_codes[seq][:, g, e_columns].bitcast(FP8X4),
+                            lhsT_scale=k_scales[seq][:, g, e_columns],
+                            rhs=v_codes[seq][:, g, d_columns].bitcast(FP8X4),
+                            rhs_scale=v_scales[seq][:, g, d_columns],
+                            start=(g == 0),
+                            stop=(g == GROUPS_PER_SEQ - 1),
+                        )
+            state[seq] = bank
+
+        def store_state(seq):
+            result = seq_pool.tile([P, HEADS, HALVES, HEAD_DIM], F32)
+            nc.scalar.copy(out=result[:], in_=state[seq][:])
+            nc.sync.dma_start(out=out[seq].rearrange("h (a j) d -> j h a d", a=HALVES), in_=result[:])
+
+        def exists(i):
+            return 0 <= i < GROUPS
+
+        for s in range(-2, GROUPS + 2):
+            done_seq, last_group = divmod(s - 2, GROUPS_PER_SEQ)
+            seq_is_done = exists(s - 2) and last_group == GROUPS_PER_SEQ - 1
+            if seq_is_done:
+                add_up_state(done_seq)
+            if exists(s + 2):
+                transpose_x(s + 2)
+            if exists(s - 1):
+                if (s - 1) % GROUPS_PER_SEQ == 0:
+                    open_sequence((s - 1) // GROUPS_PER_SEQ)
+                k_rot = rotate(s - 1)
+                quantise_v(s - 1)
+            if exists(s + 1):
+                quantise_x(s + 1)
+            if exists(s - 1):
+                quantise_k_rot(s - 1, k_rot)
+            if exists(s):
+                open_group(s)
+            for c in range(COLUMN_BLOCKS):
+                if exists(s):
+                    activate(s, c)
+                if exists(s + 1):
+                    project(s + 1, c)
+            if exists(s + 2):
+                copy_flipped(s + 2)
+            if seq_is_done:
+                store_state(done_seq)

@@ -22,6 +22,7 @@ WORD_BLOCKS = FEATURES // 2 // P
 COLUMN_BLOCKS = 2 * HEADS
 W_COLUMNS = COLUMN_BLOCKS * HEAD_DIM
 K_ROT_SCALE = 1.0 / 16.0
+RUN = 4
 
 FLOPS = 2 * SEQS * POSITIONS * FEATURES * W_COLUMNS + 2 * SEQS * HEADS * POSITIONS * HALVES * HEAD_DIM * HEAD_DIM
 
@@ -136,14 +137,18 @@ def tile_linearattention_pa_t_kernel(tc, x, w_k, w_v, cos_tab, sin_tab, out):
             banks[(i, c)] = bank
 
         def open_group(i):
-            k_tile = stream.tile([P, HEADS, HEAD_DIM, PACK], F32, name="k_act")
+            k_tile = stream.tile([P, HEADS, PACK, HEAD_DIM], F32, name="k_act")
             v_tile = stream.tile([P, HEADS, HEAD_DIM, PACK], BF16, align_bytes=64, name="v_grouped")
             k_act[i], v_grouped[i] = k_tile, v_tile
 
         def activate(i, c):
             is_v, h = divmod(c, HEADS)
-            target = v_grouped[i] if is_v else k_act[i]
-            nc.scalar.activation(out=target[:, h], in_=banks[(i, c)][:].rearrange("p t w -> p w t"), func=SILU)
+            if is_v:
+                nc.scalar.activation(
+                    out=v_grouped[i][:, h], in_=banks[(i, c)][:].rearrange("p t w -> p w t"), func=SILU
+                )
+            else:
+                nc.scalar.activation(out=k_act[i][:, h], in_=banks[(i, c)][:], func=SILU)
 
         def open_sequence(seq):
             kc = seq_pool.tile([P, GROUPS_PER_SEQ, HALVES * HEADS * HEAD_DIM], U32, align_bytes=64, name="k_codes")
@@ -157,13 +162,11 @@ def tile_linearattention_pa_t_kernel(tc, x, w_k, w_v, cos_tab, sin_tab, out):
             k_rot = stream.tile([P, HALVES, HEADS, HEAD_DIM, PACK], BF16, align_bytes=64, name="k_rot")
             for half in range(HALVES):
                 for h in range(HEADS):
-                    nc.vector.scalar_tensor_tensor(
-                        out=k_rot[:, half, h],
-                        in0=k_act[i][:, h],
-                        scalar=K_ROT_SCALE,
-                        in1=tables[g][:, half, h].rearrange("p t w -> p w t"),
-                        op0=MULT,
-                        op1=MULT,
+                    nc.vector.tensor_tensor(
+                        out=k_rot[:, half, h].rearrange("p (c r) t -> p c t r", r=RUN),
+                        in0=k_act[i][:, h].rearrange("p t (c r) -> p c t r", r=RUN),
+                        in1=tables[g][:, half, h].rearrange("p t (c r) -> p c t r", r=RUN),
+                        op=MULT,
                     )
             return k_rot
 
@@ -203,7 +206,7 @@ def tile_linearattention_pa_t_kernel(tc, x, w_k, w_v, cos_tab, sin_tab, out):
 
         def store_state(seq):
             result = seq_pool.tile([P, HEADS, HALVES, HEAD_DIM], F32)
-            nc.scalar.copy(out=result[:], in_=state[seq][:])
+            nc.scalar.mul(out=result[:], in_=state[seq][:], mul=K_ROT_SCALE)
             nc.sync.dma_start(out=out[seq].rearrange("h (a j) d -> j h a d", a=HALVES), in_=result[:])
 
         def exists(i):

@@ -10,6 +10,7 @@ U8 = mybir.dt.uint8
 FP8X4 = mybir.dt.float8_e4m3fn_x4
 SILU = mybir.ActivationFunctionType.Silu
 MULT = mybir.AluOpType.mult
+ADD = mybir.AluOpType.add
 
 SEQS, POSITIONS, FEATURES, HEADS, HEAD_DIM = 2, 4096, 512, 2, 128
 P = 128
@@ -17,6 +18,8 @@ PACK = 4
 GROUP = P * PACK
 GROUPS_PER_SEQ = POSITIONS // GROUP
 GROUPS = SEQS * GROUPS_PER_SEQ
+EARLY_GROUPS = GROUPS_PER_SEQ - 1
+PAIRS = PACK // 2
 HALVES = 2
 WORD_BLOCKS = FEATURES // 2 // P
 COLUMN_BLOCKS = 2 * HEADS
@@ -31,7 +34,7 @@ def tile_linearattention_pa_t_kernel(tc, x, w_k, w_v, cos_tab, sin_tab, out):
     nc = tc.nc
     with ExitStack() as ctx:
         const = ctx.enter_context(tc.tile_pool(name="const", bufs=1))
-        x_pool = ctx.enter_context(tc.tile_pool(name="x_rows", bufs=GROUPS))
+        x_pool = ctx.enter_context(tc.tile_pool(name="x_rows", bufs=GROUPS * PAIRS))
         table_pool = ctx.enter_context(tc.tile_pool(name="tables", bufs=GROUPS_PER_SEQ))
         seq_pool = ctx.enter_context(tc.tile_pool(name="per_sequence", bufs=SEQS))
         stream = ctx.enter_context(tc.tile_pool(name="stream", bufs=3))
@@ -44,10 +47,11 @@ def tile_linearattention_pa_t_kernel(tc, x, w_k, w_v, cos_tab, sin_tab, out):
 
         def load_x(i):
             seq, g = divmod(i, GROUPS_PER_SEQ)
-            rows = x_pool.tile([P, PACK, FEATURES], BF16)
-            positions = x[seq, g * GROUP : (g + 1) * GROUP, :]
-            nc.sync.dma_start(out=rows[:], in_=positions.rearrange("(p t) d -> p t d", t=PACK))
-            x_rows[i] = rows
+            positions = x[seq, g * GROUP : (g + 1) * GROUP, :].rearrange("(p t) d -> p t d", t=PACK)
+            for pair in range(PAIRS):
+                rows = x_pool.tile([P, 2, FEATURES], BF16)
+                nc.sync.dma_start(out=rows[:], in_=positions[:, 2 * pair : 2 * pair + 2, :])
+                x_rows[(i, pair)] = rows
 
         def load_weight(w, name):
             raw = const.tile([P, PACK, HEADS * HEAD_DIM], BF16, name=name)
@@ -64,9 +68,9 @@ def tile_linearattention_pa_t_kernel(tc, x, w_k, w_v, cos_tab, sin_tab, out):
                 nc.sync.dma_start(out=both[:, half], in_=positions.rearrange("h (p t) w -> p h t w", t=PACK))
             tables[g] = both
 
-        load_x(0)
         raw_k = load_weight(w_k, "raw_k")
         raw_v = load_weight(w_v, "raw_v")
+        load_x(0)
         for g in range(GROUPS_PER_SEQ):
             load_tables(g)
             if g + 1 < GROUPS_PER_SEQ:
@@ -86,20 +90,21 @@ def tile_linearattention_pa_t_kernel(tc, x, w_k, w_v, cos_tab, sin_tab, out):
         w_scales = const.tile([P, W_COLUMNS], U8, align_bytes=64)
         for first, raw in ((0, raw_k), (HEADS * HEAD_DIM, raw_v)):
             nc.vector.tensor_copy(
-                out=w_grouped[:, first : first + HEADS * HEAD_DIM, :], in_=raw[:].rearrange("p t c -> p c t")
+                out=w_grouped[:, first : first + HEADS * HEAD_DIM, :].rearrange("p (c r) t -> p c t r", r=RUN),
+                in_=raw[:].rearrange("p t (c r) -> p c t r", r=RUN),
             )
         nc.vector.quantize_mx(
             out=w_codes[:].bitcast(FP8X4), scales=w_scales[:], in_=w_grouped[:].rearrange("p c t -> p (c t)")
         )
 
         flipped, x_grouped, x_codes, x_scales, banks, k_act, v_grouped = {}, {}, {}, {}, {}, {}, {}
-        k_codes, k_scales, v_codes, v_scales, state = {}, {}, {}, {}, {}
+        k_codes, k_scales, v_codes, v_scales, early_sums = {}, {}, {}, {}, {}
 
         def transpose_x(i):
-            for pair in range(PACK // 2):
+            for pair in range(PAIRS):
                 bank = flip_psum.tile([P, 2, WORD_BLOCKS, P], F32, name="flip_bank")
                 for t in range(2):
-                    words = x_rows[i][:, 2 * pair + t, :].bitcast(F32)
+                    words = x_rows[(i, pair)][:, t, :].bitcast(F32)
                     for u in range(WORD_BLOCKS):
                         nc.tensor.transpose(bank[:, t, u, :], words[:, u * P : (u + 1) * P], identity[:])
                 flipped[(i, pair)] = bank
@@ -107,7 +112,7 @@ def tile_linearattention_pa_t_kernel(tc, x, w_k, w_v, cos_tab, sin_tab, out):
         def copy_flipped(i):
             grouped = stream.tile([P, GROUP * PACK], BF16, align_bytes=64, name="x_grouped")
             words = grouped[:].bitcast(F32).rearrange("q (t m u) -> q t m u", t=PACK, u=WORD_BLOCKS)
-            for pair in range(PACK // 2):
+            for pair in range(PAIRS):
                 nc.scalar.copy(
                     out=words[:, 2 * pair : 2 * pair + 2],
                     in_=flipped[(i, pair)][:].rearrange("q t u m -> q t m u"),
@@ -186,37 +191,47 @@ def tile_linearattention_pa_t_kernel(tc, x, w_k, w_v, cos_tab, sin_tab, out):
                 in_=k_rot[:].rearrange("p a h w t -> p (a h w t)"),
             )
 
-        def add_up_state(seq):
+        def add_up_state(seq, groups):
             bank = state_psum.tile([P, HEADS, HALVES, HEAD_DIM], F32, name="state_bank")
             for h in range(HEADS):
                 for half in range(HALVES):
                     e_columns = slice((half * HEADS + h) * HEAD_DIM, (half * HEADS + h + 1) * HEAD_DIM)
                     d_columns = slice(h * HEAD_DIM, (h + 1) * HEAD_DIM)
-                    for g in range(GROUPS_PER_SEQ):
+                    for g in groups:
                         nc.tensor.matmul_mx(
                             out=bank[:, h, half, :],
                             lhsT=k_codes[seq][:, g, e_columns].bitcast(FP8X4),
                             lhsT_scale=k_scales[seq][:, g, e_columns],
                             rhs=v_codes[seq][:, g, d_columns].bitcast(FP8X4),
                             rhs_scale=v_scales[seq][:, g, d_columns],
-                            start=(g == 0),
-                            stop=(g == GROUPS_PER_SEQ - 1),
+                            start=(g == groups[0]),
+                            stop=(g == groups[-1]),
                         )
-            state[seq] = bank
+            return bank
 
-        def store_state(seq):
+        def keep_early_sums(seq, bank):
+            sums = seq_pool.tile([P, HEADS, HALVES, HEAD_DIM], F32, name="early_sums")
+            nc.scalar.mul(out=sums[:], in_=bank[:], mul=K_ROT_SCALE)
+            early_sums[seq] = sums
+
+        def store_state(seq, bank):
             result = seq_pool.tile([P, HEADS, HALVES, HEAD_DIM], F32)
-            nc.scalar.mul(out=result[:], in_=state[seq][:], mul=K_ROT_SCALE)
+            nc.vector.scalar_tensor_tensor(
+                out=result[:], in0=bank[:], scalar=K_ROT_SCALE, in1=early_sums[seq][:], op0=MULT, op1=ADD
+            )
             nc.sync.dma_start(out=out[seq].rearrange("h (a j) d -> j h a d", a=HALVES), in_=result[:])
 
         def exists(i):
             return 0 <= i < GROUPS
 
         for s in range(-2, GROUPS + 2):
-            done_seq, last_group = divmod(s - 2, GROUPS_PER_SEQ)
-            seq_is_done = exists(s - 2) and last_group == GROUPS_PER_SEQ - 1
-            if seq_is_done:
-                add_up_state(done_seq)
+            seq, quantised = divmod(s - 2, GROUPS_PER_SEQ)
+            early_is_ready = exists(s - 2) and quantised == EARLY_GROUPS - 1
+            all_is_ready = exists(s - 2) and quantised == GROUPS_PER_SEQ - 1
+            if early_is_ready:
+                state_bank = add_up_state(seq, range(EARLY_GROUPS))
+            if all_is_ready:
+                state_bank = add_up_state(seq, range(EARLY_GROUPS, GROUPS_PER_SEQ))
             if exists(s + 2):
                 transpose_x(s + 2)
             if exists(s - 1):
@@ -237,5 +252,7 @@ def tile_linearattention_pa_t_kernel(tc, x, w_k, w_v, cos_tab, sin_tab, out):
                     project(s + 1, c)
             if exists(s + 2):
                 copy_flipped(s + 2)
-            if seq_is_done:
-                store_state(done_seq)
+            if early_is_ready:
+                keep_early_sums(seq, state_bank)
+            if all_is_ready:
+                store_state(seq, state_bank)

@@ -25,6 +25,7 @@ WORD_BLOCKS = FEATURES // 2 // P
 COLUMN_BLOCKS = 2 * HEADS
 W_COLUMNS = COLUMN_BLOCKS * HEAD_DIM
 K_ROT_SCALE = 1.0 / 16.0
+X_LEAD = 3
 RUN = 4
 
 FLOPS = 2 * SEQS * POSITIONS * FEATURES * W_COLUMNS + 2 * SEQS * HEADS * POSITIONS * HALVES * HEAD_DIM * HEAD_DIM
@@ -68,14 +69,15 @@ def tile_linearattention_pa_t_kernel(tc, x, w_k, w_v, cos_tab, sin_tab, out):
                 nc.sync.dma_start(out=both[:, half], in_=positions.rearrange("h (p t) w -> p h t w", t=PACK))
             tables[g] = both
 
+        load_x(0)
         raw_k = load_weight(w_k, "raw_k")
         raw_v = load_weight(w_v, "raw_v")
-        load_x(0)
+        for i in range(1, X_LEAD):
+            load_x(i)
         for g in range(GROUPS_PER_SEQ):
             load_tables(g)
-            if g + 1 < GROUPS_PER_SEQ:
-                load_x(g + 1)
-        for i in range(GROUPS_PER_SEQ, GROUPS):
+            load_x(g + X_LEAD)
+        for i in range(GROUPS_PER_SEQ + X_LEAD, GROUPS):
             load_x(i)
 
         identity = const.tile([P, P], F32)

@@ -26,7 +26,7 @@ COLUMN_BLOCKS = 2 * HEADS
 W_COLUMNS = COLUMN_BLOCKS * HEAD_DIM
 K_ROT_SCALE = 1.0 / 16.0
 X_LEAD = 3
-RUN = 4
+RUN = 8
 
 FLOPS = 2 * SEQS * POSITIONS * FEATURES * W_COLUMNS + 2 * SEQS * HEADS * POSITIONS * HALVES * HEAD_DIM * HEAD_DIM
 

@@ -10,7 +10,6 @@ U8 = mybir.dt.uint8
 FP8X4 = mybir.dt.float8_e4m3fn_x4
 SILU = mybir.ActivationFunctionType.Silu
 MULT = mybir.AluOpType.mult
-ADD = mybir.AluOpType.add
 
 SEQS, POSITIONS, FEATURES, HEADS, HEAD_DIM = 2, 4096, 512, 2, 128
 P = 128
@@ -18,14 +17,12 @@ PACK = 4
 GROUP = P * PACK
 GROUPS_PER_SEQ = POSITIONS // GROUP
 GROUPS = SEQS * GROUPS_PER_SEQ
-EARLY_GROUPS = GROUPS_PER_SEQ - 1
 PAIRS = PACK // 2
 HALVES = 2
 WORD_BLOCKS = FEATURES // 2 // P
-COLUMN_BLOCKS = 2 * HEADS
-W_COLUMNS = COLUMN_BLOCKS * HEAD_DIM
+INNER = HEADS * HEAD_DIM
+W_COLUMNS = 2 * INNER
 K_ROT_SCALE = 1.0 / 16.0
-X_LEAD = 3
 RUN = 8
 
 FLOPS = 2 * SEQS * POSITIONS * FEATURES * W_COLUMNS + 2 * SEQS * HEADS * POSITIONS * HALVES * HEAD_DIM * HEAD_DIM
@@ -39,46 +36,50 @@ def tile_linearattention_pa_t_kernel(tc, x, w_k, w_v, cos_tab, sin_tab, out):
         table_pool = ctx.enter_context(tc.tile_pool(name="tables", bufs=GROUPS_PER_SEQ))
         seq_pool = ctx.enter_context(tc.tile_pool(name="per_sequence", bufs=SEQS))
         stream = ctx.enter_context(tc.tile_pool(name="stream", bufs=3))
-        flip_psum = ctx.enter_context(tc.psum_pool(name="flip_psum", bufs=3))
-        proj_psum = ctx.enter_context(tc.psum_pool(name="proj_psum", bufs=COLUMN_BLOCKS))
+        single = ctx.enter_context(tc.tile_pool(name="single", bufs=1))
+        flip_psum = ctx.enter_context(tc.psum_pool(name="flip_psum", bufs=2))
+        v_psum = ctx.enter_context(tc.psum_pool(name="v_psum", bufs=2))
+        k_psum = ctx.enter_context(tc.psum_pool(name="k_psum", bufs=1))
         state_psum = ctx.enter_context(tc.psum_pool(name="state_psum", bufs=1))
         ctx.enter_context(tc.manual_schedule())
 
         x_rows, tables = {}, {}
 
-        def load_x(i):
+        def load_x(i, pair):
             seq, g = divmod(i, GROUPS_PER_SEQ)
             positions = x[seq, g * GROUP : (g + 1) * GROUP, :].rearrange("(p t) d -> p t d", t=PACK)
-            for pair in range(PAIRS):
-                rows = x_pool.tile([P, 2, FEATURES], BF16)
-                nc.sync.dma_start(out=rows[:], in_=positions[:, 2 * pair : 2 * pair + 2, :])
-                x_rows[(i, pair)] = rows
+            rows = x_pool.tile([P, 2, FEATURES], BF16)
+            nc.sync.dma_start(out=rows[:], in_=positions[:, 2 * pair : 2 * pair + 2, :])
+            x_rows[(i, pair)] = rows
 
         def load_weight(w, name):
-            raw = const.tile([P, PACK, HEADS * HEAD_DIM], BF16, name=name)
+            raw = const.tile([P, PACK, INNER], BF16, name=name)
             nc.sync.dma_start(
                 out=raw[:].rearrange("q (u e) c -> q u (e c)", e=2),
                 in_=w.rearrange("(u q e) c -> q u (e c)", u=WORD_BLOCKS, e=2),
             )
             return raw
 
-        def load_tables(g):
-            both = table_pool.tile([P, HALVES, HEADS, PACK, HEAD_DIM], BF16)
-            for half, table in enumerate((cos_tab, sin_tab)):
-                positions = table[:, g * GROUP : (g + 1) * GROUP, :]
-                nc.sync.dma_start(out=both[:, half], in_=positions.rearrange("h (p t) w -> p h t w", t=PACK))
-            tables[g] = both
+        def load_table(g, half):
+            if half == 0:
+                tables[g] = table_pool.tile([P, HALVES, HEADS, PACK, HEAD_DIM], BF16, name="table")
+            positions = (cos_tab, sin_tab)[half][:, g * GROUP : (g + 1) * GROUP, :]
+            nc.sync.dma_start(out=tables[g][:, half], in_=positions.rearrange("h (p t) w -> p h t w", t=PACK))
 
-        load_x(0)
+        load_x(0, 0)
         raw_k = load_weight(w_k, "raw_k")
+        load_x(0, 1)
         raw_v = load_weight(w_v, "raw_v")
-        for i in range(1, X_LEAD):
-            load_x(i)
-        for g in range(GROUPS_PER_SEQ):
-            load_tables(g)
-            load_x(g + X_LEAD)
-        for i in range(GROUPS_PER_SEQ + X_LEAD, GROUPS):
-            load_x(i)
+        load_x(1, 0)
+        load_table(0, 0)
+        load_x(1, 1)
+        load_table(0, 1)
+        for i in range(2, GROUPS):
+            for pair in range(PAIRS):
+                load_x(i, pair)
+            if i - 1 < GROUPS_PER_SEQ:
+                for half in range(HALVES):
+                    load_table(i - 1, half)
 
         identity = const.tile([P, P], F32)
         make_identity(nc, identity[:])
@@ -87,95 +88,130 @@ def tile_linearattention_pa_t_kernel(tc, x, w_k, w_v, cos_tab, sin_tab, out):
         nc.vector.memset(zero[:], 0.0)
         nc.scalar.activation(out=unused[:], in_=zero[:], func=SILU)
 
-        w_grouped = const.tile([P, W_COLUMNS, PACK], BF16, align_bytes=64)
         w_codes = const.tile([P, W_COLUMNS], U32, align_bytes=64)
         w_scales = const.tile([P, W_COLUMNS], U8, align_bytes=64)
-        for first, raw in ((0, raw_k), (HEADS * HEAD_DIM, raw_v)):
+
+        def quantise_weight(raw, first, name):
+            grouped = const.tile([P, INNER, PACK], BF16, align_bytes=64, name=name)
             nc.vector.tensor_copy(
-                out=w_grouped[:, first : first + HEADS * HEAD_DIM, :].rearrange("p (c r) t -> p c t r", r=RUN),
+                out=grouped[:].rearrange("p (c r) t -> p c t r", r=RUN),
                 in_=raw[:].rearrange("p t (c r) -> p c t r", r=RUN),
             )
-        nc.vector.quantize_mx(
-            out=w_codes[:].bitcast(FP8X4), scales=w_scales[:], in_=w_grouped[:].rearrange("p c t -> p (c t)")
-        )
+            nc.vector.quantize_mx(
+                out=w_codes[:, first : first + INNER].bitcast(FP8X4),
+                scales=w_scales[:, first : first + INNER],
+                in_=grouped[:].rearrange("p c t -> p (c t)"),
+            )
 
-        flipped, x_grouped, x_codes, x_scales, banks, k_act, v_grouped = {}, {}, {}, {}, {}, {}, {}
-        k_codes, k_scales, v_codes, v_scales, early_sums = {}, {}, {}, {}, {}
+        flipped, x_grouped, x_codes, x_scales, k_banks, k_flipped_banks, v_banks = {}, {}, {}, {}, {}, {}, {}
+        k_flipped, k_act, v_grouped, k_rot = {}, {}, {}, {}
+        k_codes, k_scales, v_codes, v_scales = {}, {}, {}, {}
 
-        def transpose_x(i):
-            for pair in range(PAIRS):
-                bank = flip_psum.tile([P, 2, WORD_BLOCKS, P], F32, name="flip_bank")
-                for t in range(2):
-                    words = x_rows[(i, pair)][:, t, :].bitcast(F32)
-                    for u in range(WORD_BLOCKS):
-                        nc.tensor.transpose(bank[:, t, u, :], words[:, u * P : (u + 1) * P], identity[:])
-                flipped[(i, pair)] = bank
+        def transpose_x(i, pair):
+            bank = flip_psum.tile([P, 2, WORD_BLOCKS, P], F32, name="flip_bank")
+            for t in range(2):
+                words = x_rows[(i, pair)][:, t, :].bitcast(F32)
+                for u in range(WORD_BLOCKS):
+                    nc.tensor.transpose(bank[:, t, u, :], words[:, u * P : (u + 1) * P], identity[:])
+            flipped[(i, pair)] = bank
 
-        def copy_flipped(i):
-            grouped = stream.tile([P, GROUP * PACK], BF16, align_bytes=64, name="x_grouped")
-            words = grouped[:].bitcast(F32).rearrange("q (t m u) -> q t m u", t=PACK, u=WORD_BLOCKS)
-            for pair in range(PAIRS):
-                nc.scalar.copy(
-                    out=words[:, 2 * pair : 2 * pair + 2],
-                    in_=flipped[(i, pair)][:].rearrange("q t u m -> q t m u"),
-                )
-            x_grouped[i] = grouped
+        def copy_flipped(i, pair):
+            if pair == 0:
+                x_grouped[i] = stream.tile([P, GROUP * PACK], BF16, align_bytes=64, name="x_grouped")
+            words = x_grouped[i][:].bitcast(F32).rearrange("q (t m u) -> q t m u", t=PACK, u=WORD_BLOCKS)
+            nc.scalar.copy(
+                out=words[:, 2 * pair : 2 * pair + 2],
+                in_=flipped[(i, pair)][:].rearrange("q t u m -> q t m u"),
+            )
 
-        def quantise_x(i):
+        def open_x_codes(i):
             codes = stream.tile([P, GROUP], U32, align_bytes=64, name="x_codes")
             scales = stream.tile([P, GROUP], U8, align_bytes=64, name="x_scales")
-            nc.vector.quantize_mx(out=codes[:].bitcast(FP8X4), scales=scales[:], in_=x_grouped[i][:])
             x_codes[i], x_scales[i] = codes, scales
 
-        def project(i, c):
-            bank = proj_psum.tile([P, PACK, HEAD_DIM], F32, name="proj_bank")
-            columns = slice(c * HEAD_DIM, (c + 1) * HEAD_DIM)
+        def quantise_x(i, first, last):
+            nc.vector.quantize_mx(
+                out=x_codes[i][:, first:last].bitcast(FP8X4),
+                scales=x_scales[i][:, first:last],
+                in_=x_grouped[i][:, first * PACK : last * PACK],
+            )
+
+        def multiply(bank_columns, i, t, columns):
+            rows = slice(t * P, (t + 1) * P)
+            nc.tensor.matmul_mx(
+                out=bank_columns,
+                lhsT=x_codes[i][:, rows].bitcast(FP8X4),
+                lhsT_scale=x_scales[i][:, rows],
+                rhs=w_codes[:, columns].bitcast(FP8X4),
+                rhs_scale=w_scales[:, columns],
+                start=True,
+                stop=True,
+            )
+
+        def project_k_flipped(i):
+            bank = k_psum.tile([P, GROUP], F32, name="k_flipped_bank")
+            nc.tensor.matmul_mx(
+                out=bank[:],
+                lhsT=w_codes[:, 0:HEAD_DIM].bitcast(FP8X4),
+                lhsT_scale=w_scales[:, 0:HEAD_DIM],
+                rhs=x_codes[i][:].bitcast(FP8X4),
+                rhs_scale=x_scales[i][:],
+                start=True,
+                stop=True,
+            )
+            k_flipped_banks[i] = bank
+
+        def project_k(i):
+            bank = k_psum.tile([P, PACK, HEAD_DIM], F32, name="k_bank")
             for t in range(PACK):
-                rows = slice(t * P, (t + 1) * P)
-                nc.tensor.matmul_mx(
-                    out=bank[:, t, :],
-                    lhsT=x_codes[i][:, rows].bitcast(FP8X4),
-                    lhsT_scale=x_scales[i][:, rows],
-                    rhs=w_codes[:, columns].bitcast(FP8X4),
-                    rhs_scale=w_scales[:, columns],
-                    start=True,
-                    stop=True,
-                )
-            banks[(i, c)] = bank
+                multiply(bank[:, t, :], i, t, slice(HEAD_DIM, INNER))
+            k_banks[i] = bank
 
-        def open_group(i):
-            k_tile = stream.tile([P, HEADS, PACK, HEAD_DIM], F32, name="k_act")
-            v_tile = stream.tile([P, HEADS, HEAD_DIM, PACK], BF16, align_bytes=64, name="v_grouped")
-            k_act[i], v_grouped[i] = k_tile, v_tile
+        def project_v(i, h):
+            bank = v_psum.tile([P, PACK, HEAD_DIM], F32, name="v_bank")
+            for t in range(PACK):
+                multiply(bank[:, t, :], i, t, slice(INNER + h * HEAD_DIM, INNER + (h + 1) * HEAD_DIM))
+            v_banks[(i, h)] = bank
 
-        def activate(i, c):
-            is_v, h = divmod(c, HEADS)
-            if is_v:
-                nc.scalar.activation(
-                    out=v_grouped[i][:, h], in_=banks[(i, c)][:].rearrange("p t w -> p w t"), func=SILU
-                )
-            else:
-                nc.scalar.activation(out=k_act[i][:, h], in_=banks[(i, c)][:], func=SILU)
+        def activate_k_flipped(i):
+            k_flipped[i] = stream.tile([P, PACK, P], F32, name="k_flipped")
+            nc.scalar.activation(
+                out=k_flipped[i][:], in_=k_flipped_banks[i][:].rearrange("j (t p) -> j t p", t=PACK), func=SILU
+            )
+
+        def activate_k(i):
+            k_act[(i, 1)] = stream.tile([P, PACK, HEAD_DIM], F32, name="k_act")
+            nc.scalar.activation(out=k_act[(i, 1)][:], in_=k_banks[i][:], func=SILU)
+
+        def turn_k(i):
+            bank = k_psum.tile([P, PACK, HEAD_DIM], F32, name="k_turned")
+            for t in range(PACK):
+                nc.tensor.transpose(bank[:, t, :], k_flipped[i][:, t, :], identity[:])
+            k_act[(i, 0)] = bank
+
+        def activate_v(i, h):
+            if h == 0:
+                v_grouped[i] = stream.tile([P, HEADS, HEAD_DIM, PACK], BF16, align_bytes=64, name="v_grouped")
+            nc.scalar.activation(out=v_grouped[i][:, h], in_=v_banks[(i, h)][:].rearrange("p t w -> p w t"), func=SILU)
 
         def open_sequence(seq):
-            kc = seq_pool.tile([P, GROUPS_PER_SEQ, HALVES * HEADS * HEAD_DIM], U32, align_bytes=64, name="k_codes")
-            ks = seq_pool.tile([P, GROUPS_PER_SEQ, HALVES * HEADS * HEAD_DIM], U8, align_bytes=64, name="k_scales")
-            vc = seq_pool.tile([P, GROUPS_PER_SEQ, HEADS * HEAD_DIM], U32, align_bytes=64, name="v_codes")
-            vs = seq_pool.tile([P, GROUPS_PER_SEQ, HEADS * HEAD_DIM], U8, align_bytes=64, name="v_scales")
+            kc = seq_pool.tile([P, GROUPS_PER_SEQ, HALVES * INNER], U32, align_bytes=64, name="k_codes")
+            ks = seq_pool.tile([P, GROUPS_PER_SEQ, HALVES * INNER], U8, align_bytes=64, name="k_scales")
+            vc = seq_pool.tile([P, GROUPS_PER_SEQ, INNER], U32, align_bytes=64, name="v_codes")
+            vs = seq_pool.tile([P, GROUPS_PER_SEQ, INNER], U8, align_bytes=64, name="v_scales")
             k_codes[seq], k_scales[seq], v_codes[seq], v_scales[seq] = kc, ks, vc, vs
 
-        def rotate(i):
-            g = i % GROUPS_PER_SEQ
-            k_rot = stream.tile([P, HALVES, HEADS, HEAD_DIM, PACK], BF16, align_bytes=64, name="k_rot")
-            for half in range(HALVES):
-                for h in range(HEADS):
-                    nc.vector.tensor_tensor(
-                        out=k_rot[:, half, h].rearrange("p (c r) t -> p c t r", r=RUN),
-                        in0=k_act[i][:, h].rearrange("p t (c r) -> p c t r", r=RUN),
-                        in1=tables[g][:, half, h].rearrange("p t (c r) -> p c t r", r=RUN),
-                        op=MULT,
-                    )
-            return k_rot
+        def open_k_rot(i):
+            k_rot[(i, 0)] = stream.tile([P, HALVES, HEAD_DIM, PACK], BF16, align_bytes=64, name="k_rot_0")
+            k_rot[(i, 1)] = single.tile([P, HALVES, HEAD_DIM, PACK], BF16, align_bytes=64, name="k_rot_1")
+
+        def rotate(engine, i, h, half):
+            engine.tensor_tensor(
+                out=k_rot[(i, h)][:, half].rearrange("p (c r) t -> p c t r", r=RUN),
+                in0=k_act[(i, h)][:].rearrange("p t (c r) -> p c t r", r=RUN),
+                in1=tables[i % GROUPS_PER_SEQ][:, half, h].rearrange("p t (c r) -> p c t r", r=RUN),
+                op=MULT,
+            )
 
         def quantise_v(i):
             seq, g = divmod(i, GROUPS_PER_SEQ)
@@ -185,76 +221,112 @@ def tile_linearattention_pa_t_kernel(tc, x, w_k, w_v, cos_tab, sin_tab, out):
                 in_=v_grouped[i][:].rearrange("p h w t -> p (h w t)"),
             )
 
-        def quantise_k_rot(i, k_rot):
+        def quantise_k_rot(i, h):
             seq, g = divmod(i, GROUPS_PER_SEQ)
+            columns = slice(h * HALVES * HEAD_DIM, (h + 1) * HALVES * HEAD_DIM)
             nc.vector.quantize_mx(
-                out=k_codes[seq][:, g, :].bitcast(FP8X4),
-                scales=k_scales[seq][:, g, :],
-                in_=k_rot[:].rearrange("p a h w t -> p (a h w t)"),
+                out=k_codes[seq][:, g, columns].bitcast(FP8X4),
+                scales=k_scales[seq][:, g, columns],
+                in_=k_rot[(i, h)][:].rearrange("p a c t -> p (a c t)"),
             )
 
-        def add_up_state(seq, groups):
-            bank = state_psum.tile([P, HEADS, HALVES, HEAD_DIM], F32, name="state_bank")
+        def add_up(block, seq, h, half, groups, first, last):
+            e_columns = slice((h * HALVES + half) * HEAD_DIM, (h * HALVES + half + 1) * HEAD_DIM)
+            d_columns = slice(h * HEAD_DIM, (h + 1) * HEAD_DIM)
+            for g in groups:
+                nc.tensor.matmul_mx(
+                    out=block,
+                    lhsT=k_codes[seq][:, g, e_columns].bitcast(FP8X4),
+                    lhsT_scale=k_scales[seq][:, g, e_columns],
+                    rhs=v_codes[seq][:, g, d_columns].bitcast(FP8X4),
+                    rhs_scale=v_scales[seq][:, g, d_columns],
+                    start=(g == first),
+                    stop=(g == last),
+                )
+
+        LAST = GROUPS_PER_SEQ - 1
+
+        quantise_weight(raw_k, 0, "k_grouped")
+        open_x_codes(0)
+        for pair in range(PAIRS):
+            transpose_x(0, pair)
+            copy_flipped(0, pair)
+            quantise_x(0, pair * GROUP // 2, (pair + 1) * GROUP // 2)
+        project_k(0)
+        project_k_flipped(0)
+        activate_k(0)
+        activate_k_flipped(0)
+        turn_k(0)
+        for pair in range(PAIRS):
+            transpose_x(1, pair)
+            copy_flipped(1, pair)
+        quantise_weight(raw_v, INNER, "w_v_grouped")
+        for h in range(HEADS):
+            project_v(0, h)
+
+        blocks = [(h, half) for h in range(HEADS) for half in range(HALVES)]
+        for i in range(GROUPS):
+            seq, g = divmod(i, GROUPS_PER_SEQ)
+            more = i + 1 < GROUPS
+            if g == 0:
+                open_sequence(seq)
+            open_k_rot(i)
+            if i + 2 < GROUPS:
+                for pair in range(PAIRS):
+                    transpose_x(i + 2, pair)
+            rotate(nc.gpsimd, i, 1, 1)
+            if i == 0:
+                rotate(nc.vector, i, 1, 0)
+            if more:
+                open_x_codes(i + 1)
+                quantise_x(i + 1, 0, GROUP)
+                project_k_flipped(i + 1)
+                project_k(i + 1)
+            rotate(nc.vector, i, 0, 0)
+            rotate(nc.vector, i, 0, 1)
+            if i > 0:
+                rotate(nc.vector, i, 1, 0)
             for h in range(HEADS):
-                for half in range(HALVES):
-                    e_columns = slice((half * HEADS + h) * HEAD_DIM, (half * HEADS + h + 1) * HEAD_DIM)
-                    d_columns = slice(h * HEAD_DIM, (h + 1) * HEAD_DIM)
-                    for g in groups:
-                        nc.tensor.matmul_mx(
-                            out=bank[:, h, half, :],
-                            lhsT=k_codes[seq][:, g, e_columns].bitcast(FP8X4),
-                            lhsT_scale=k_scales[seq][:, g, e_columns],
-                            rhs=v_codes[seq][:, g, d_columns].bitcast(FP8X4),
-                            rhs_scale=v_scales[seq][:, g, d_columns],
-                            start=(g == groups[0]),
-                            stop=(g == groups[-1]),
-                        )
-            return bank
+                activate_v(i, h)
+                if more:
+                    project_v(i + 1, h)
+            if i + 2 < GROUPS:
+                copy_flipped(i + 2, 0)
+            if more:
+                activate_k_flipped(i + 1)
+                turn_k(i + 1)
+                activate_k(i + 1)
+            if i + 2 < GROUPS:
+                copy_flipped(i + 2, 1)
+            quantise_v(i)
+            if more:
+                quantise_k_rot(i, 0)
+                quantise_k_rot(i, 1)
+            if seq == 1 and g < len(blocks):
+                h, half = blocks[g]
+                if g == 0:
+                    state_bank = state_psum.tile([P, HEADS, HALVES, HEAD_DIM], F32, name="state_bank")
+                add_up(state_bank[:, h, half, :], 0, h, half, range(GROUPS_PER_SEQ), 0, LAST)
+            if seq == 1 and g == len(blocks):
+                result = seq_pool.tile([P, HEADS, HALVES, HEAD_DIM], F32, name="result")
+                nc.scalar.mul(out=result[:], in_=state_bank[:], mul=K_ROT_SCALE)
+                nc.sync.dma_start(out=out[0].rearrange("h (a j) d -> j h a d", a=HALVES), in_=result[:])
 
-        def keep_early_sums(seq, bank):
-            sums = seq_pool.tile([P, HEADS, HALVES, HEAD_DIM], F32, name="early_sums")
-            nc.scalar.mul(out=sums[:], in_=bank[:], mul=K_ROT_SCALE)
-            early_sums[seq] = sums
-
-        def store_state(seq, bank):
-            result = seq_pool.tile([P, HEADS, HALVES, HEAD_DIM], F32)
-            nc.vector.scalar_tensor_tensor(
-                out=result[:], in0=bank[:], scalar=K_ROT_SCALE, in1=early_sums[seq][:], op0=MULT, op1=ADD
-            )
-            nc.sync.dma_start(out=out[seq].rearrange("h (a j) d -> j h a d", a=HALVES), in_=result[:])
-
-        def exists(i):
-            return 0 <= i < GROUPS
-
-        for s in range(-2, GROUPS + 2):
-            seq, quantised = divmod(s - 2, GROUPS_PER_SEQ)
-            early_is_ready = exists(s - 2) and quantised == EARLY_GROUPS - 1
-            all_is_ready = exists(s - 2) and quantised == GROUPS_PER_SEQ - 1
-            if early_is_ready:
-                state_bank = add_up_state(seq, range(EARLY_GROUPS))
-            if all_is_ready:
-                state_bank = add_up_state(seq, range(EARLY_GROUPS, GROUPS_PER_SEQ))
-            if exists(s + 2):
-                transpose_x(s + 2)
-            if exists(s - 1):
-                if (s - 1) % GROUPS_PER_SEQ == 0:
-                    open_sequence((s - 1) // GROUPS_PER_SEQ)
-                k_rot = rotate(s - 1)
-                quantise_v(s - 1)
-            if exists(s + 1):
-                quantise_x(s + 1)
-            if exists(s - 1):
-                quantise_k_rot(s - 1, k_rot)
-            if exists(s):
-                open_group(s)
-            for c in range(COLUMN_BLOCKS):
-                if exists(s):
-                    activate(s, c)
-                if exists(s + 1):
-                    project(s + 1, c)
-            if exists(s + 2):
-                copy_flipped(s + 2)
-            if early_is_ready:
-                keep_early_sums(seq, state_bank)
-            if all_is_ready:
-                store_state(seq, state_bank)
+        i, seq = GROUPS - 1, SEQS - 1
+        open_blocks = {}
+        for n, (h, half) in enumerate(blocks):
+            if n == 0:
+                bank = state_psum.tile([P, PACK, HEAD_DIM], F32, name="state_bank")
+            elif n < 3:
+                bank = flip_psum.tile([P, PACK, HEAD_DIM], F32, name="flip_bank")
+            else:
+                bank = k_psum.tile([P, PACK, HEAD_DIM], F32, name="k_bank")
+            open_blocks[(h, half)] = bank[:, 0, :]
+            add_up(open_blocks[(h, half)], seq, h, half, range(LAST), 0, LAST)
+        result = seq_pool.tile([P, HEADS, HALVES, HEAD_DIM], F32, name="result")
+        for h in range(HEADS):
+            quantise_k_rot(i, h)
+            for half in range(HALVES):
+                add_up(open_blocks[(h, half)], seq, h, half, [LAST], 0, LAST)
+                nc.scalar.mul(out=result[:, h, half, :], in_=open_blocks[(h, half)], mul=K_ROT_SCALE)
+            nc.sync.dma_start(out=out[seq, h].rearrange("(a j) d -> j a d", a=HALVES), in_=result[:, h])

@@ -24,6 +24,7 @@ INNER = HEADS * HEAD_DIM
 W_COLUMNS = 2 * INNER
 K_ROT_SCALE = 1.0 / 16.0
 RUN = 8
+GPSIMD_COLUMNS = 96
 
 FLOPS = 2 * SEQS * POSITIONS * FEATURES * W_COLUMNS + 2 * SEQS * HEADS * POSITIONS * HALVES * HEAD_DIM * HEAD_DIM
 
@@ -69,8 +70,8 @@ def tile_linearattention_pa_t_kernel(tc, x, w_k, w_v, cos_tab, sin_tab, out):
         load_x(0, 0)
         raw_k = load_weight(w_k, "raw_k")
         load_x(0, 1)
-        raw_v = load_weight(w_v, "raw_v")
         load_x(1, 0)
+        raw_v = load_weight(w_v, "raw_v")
         load_table(0, 0)
         load_x(1, 1)
         load_table(0, 1)
@@ -205,11 +206,17 @@ def tile_linearattention_pa_t_kernel(tc, x, w_k, w_v, cos_tab, sin_tab, out):
             k_rot[(i, 0)] = stream.tile([P, HALVES, HEAD_DIM, PACK], BF16, align_bytes=64, name="k_rot_0")
             k_rot[(i, 1)] = single.tile([P, HALVES, HEAD_DIM, PACK], BF16, align_bytes=64, name="k_rot_1")
 
-        def rotate(engine, i, h, half):
+        def rotate_on_vector(i):
+            rotate(nc.vector, i, 0, 0, 0, HEAD_DIM)
+            rotate(nc.vector, i, 0, 1, 0, HEAD_DIM)
+            rotate(nc.vector, i, 1, 0, 0, HEAD_DIM)
+            rotate(nc.vector, i, 1, 1, GPSIMD_COLUMNS, HEAD_DIM)
+
+        def rotate(engine, i, h, half, first, last):
             engine.tensor_tensor(
-                out=k_rot[(i, h)][:, half].rearrange("p (c r) t -> p c t r", r=RUN),
-                in0=k_act[(i, h)][:].rearrange("p t (c r) -> p c t r", r=RUN),
-                in1=tables[i % GROUPS_PER_SEQ][:, half, h].rearrange("p t (c r) -> p c t r", r=RUN),
+                out=k_rot[(i, h)][:, half, first:last].rearrange("p (c r) t -> p c t r", r=RUN),
+                in0=k_act[(i, h)][:, :, first:last].rearrange("p t (c r) -> p c t r", r=RUN),
+                in1=tables[i % GROUPS_PER_SEQ][:, half, h, :, first:last].rearrange("p t (c r) -> p c t r", r=RUN),
                 op=MULT,
             )
 
@@ -252,14 +259,15 @@ def tile_linearattention_pa_t_kernel(tc, x, w_k, w_v, cos_tab, sin_tab, out):
             transpose_x(0, pair)
             copy_flipped(0, pair)
             quantise_x(0, pair * GROUP // 2, (pair + 1) * GROUP // 2)
-        project_k(0)
+        transpose_x(1, 0)
+        copy_flipped(1, 0)
         project_k_flipped(0)
-        activate_k(0)
+        project_k(0)
         activate_k_flipped(0)
+        activate_k(0)
+        transpose_x(1, 1)
+        copy_flipped(1, 1)
         turn_k(0)
-        for pair in range(PAIRS):
-            transpose_x(1, pair)
-            copy_flipped(1, pair)
         quantise_weight(raw_v, INNER, "w_v_grouped")
         for h in range(HEADS):
             project_v(0, h)
@@ -274,18 +282,16 @@ def tile_linearattention_pa_t_kernel(tc, x, w_k, w_v, cos_tab, sin_tab, out):
             if i + 2 < GROUPS:
                 for pair in range(PAIRS):
                     transpose_x(i + 2, pair)
-            rotate(nc.gpsimd, i, 1, 1)
+            rotate(nc.gpsimd, i, 1, 1, 0, GPSIMD_COLUMNS)
             if i == 0:
-                rotate(nc.vector, i, 1, 0)
+                rotate_on_vector(i)
             if more:
                 open_x_codes(i + 1)
                 quantise_x(i + 1, 0, GROUP)
                 project_k_flipped(i + 1)
                 project_k(i + 1)
-            rotate(nc.vector, i, 0, 0)
-            rotate(nc.vector, i, 0, 1)
             if i > 0:
-                rotate(nc.vector, i, 1, 0)
+                rotate_on_vector(i)
             for h in range(HEADS):
                 activate_v(i, h)
                 if more:

@@ -271,43 +271,50 @@ def tile_linearattention_pa_t_kernel(tc, x, w_k, w_v, cos_tab, sin_tab, out):
         quantise_weight(raw_v, INNER, "w_v_grouped")
         for h in range(HEADS):
             project_v(0, h)
+            activate_v(0, h)
+        for pair in range(PAIRS):
+            transpose_x(2, pair)
+            copy_flipped(2, pair)
+
+        def quantise_and_project(i):
+            open_x_codes(i)
+            quantise_x(i, 0, GROUP)
+            project_k_flipped(i)
+            project_k(i)
+            for h in range(HEADS):
+                project_v(i, h)
 
         blocks = [(h, half) for h in range(HEADS) for half in range(HALVES)]
         for i in range(GROUPS):
             seq, g = divmod(i, GROUPS_PER_SEQ)
-            more = i + 1 < GROUPS
             if g == 0:
                 open_sequence(seq)
             open_k_rot(i)
-            if i + 2 < GROUPS:
+            if i + 3 < GROUPS:
                 for pair in range(PAIRS):
-                    transpose_x(i + 2, pair)
+                    transpose_x(i + 3, pair)
             rotate(nc.gpsimd, i, 1, 1, 0, GPSIMD_COLUMNS)
+            rotate_on_vector(i)
             if i == 0:
-                rotate_on_vector(i)
-            if more:
-                open_x_codes(i + 1)
-                quantise_x(i + 1, 0, GROUP)
-                project_k_flipped(i + 1)
-                project_k(i + 1)
-            if i > 0:
-                rotate_on_vector(i)
-            for h in range(HEADS):
-                activate_v(i, h)
-                if more:
-                    project_v(i + 1, h)
-            if i + 2 < GROUPS:
-                copy_flipped(i + 2, 0)
-            if more:
+                quantise_and_project(1)
+            if i + 1 < GROUPS:
                 activate_k_flipped(i + 1)
                 turn_k(i + 1)
                 activate_k(i + 1)
+                for h in range(HEADS):
+                    activate_v(i + 1, h)
+            if i + 3 < GROUPS:
+                for pair in range(PAIRS):
+                    copy_flipped(i + 3, pair)
+            if i == 0:
+                quantise_v(i)
             if i + 2 < GROUPS:
-                copy_flipped(i + 2, 1)
-            quantise_v(i)
-            if more:
-                quantise_k_rot(i, 0)
-                quantise_k_rot(i, 1)
+                quantise_and_project(i + 2)
+            if i > 0:
+                quantise_v(i)
+            if i + 1 < GROUPS:
+                for h in range(HEADS):
+                    quantise_k_rot(i, h)
             if seq == 1 and g < len(blocks):
                 h, half = blocks[g]
                 if g == 0:

@@ -33,7 +33,7 @@ def tile_linearattention_pa_t_kernel(tc, x, w_k, w_v, cos_tab, sin_tab, out):
     nc = tc.nc
     with ExitStack() as ctx:
         const = ctx.enter_context(tc.tile_pool(name="const", bufs=1))
-        x_pool = ctx.enter_context(tc.tile_pool(name="x_rows", bufs=GROUPS * PAIRS))
+        x_pool = ctx.enter_context(tc.tile_pool(name="x_rows", bufs=GROUPS))
         table_pool = ctx.enter_context(tc.tile_pool(name="tables", bufs=GROUPS_PER_SEQ))
         seq_pool = ctx.enter_context(tc.tile_pool(name="per_sequence", bufs=SEQS))
         stream = ctx.enter_context(tc.tile_pool(name="stream", bufs=3))
@@ -46,12 +46,12 @@ def tile_linearattention_pa_t_kernel(tc, x, w_k, w_v, cos_tab, sin_tab, out):
 
         x_rows, tables = {}, {}
 
-        def load_x(i, pair):
+        def load_x(i, first, last):
             seq, g = divmod(i, GROUPS_PER_SEQ)
             positions = x[seq, g * GROUP : (g + 1) * GROUP, :].rearrange("(p t) d -> p t d", t=PACK)
-            rows = x_pool.tile([P, 2, FEATURES], BF16)
-            nc.sync.dma_start(out=rows[:], in_=positions[:, 2 * pair : 2 * pair + 2, :])
-            x_rows[(i, pair)] = rows
+            if first == 0:
+                x_rows[i] = x_pool.tile([P, PACK, FEATURES], BF16, name="rows")
+            nc.sync.dma_start(out=x_rows[i][:, first:last, :], in_=positions[:, first:last, :])
 
         def load_weight(w, name):
             raw = const.tile([P, PACK, INNER], BF16, name=name)
@@ -67,17 +67,16 @@ def tile_linearattention_pa_t_kernel(tc, x, w_k, w_v, cos_tab, sin_tab, out):
             positions = (cos_tab, sin_tab)[half][:, g * GROUP : (g + 1) * GROUP, :]
             nc.sync.dma_start(out=tables[g][:, half], in_=positions.rearrange("h (p t) w -> p h t w", t=PACK))
 
-        load_x(0, 0)
+        load_x(0, 0, 2)
         raw_k = load_weight(w_k, "raw_k")
-        load_x(0, 1)
-        load_x(1, 0)
+        load_x(0, 2, PACK)
+        load_x(1, 0, 2)
         raw_v = load_weight(w_v, "raw_v")
         load_table(0, 0)
-        load_x(1, 1)
+        load_x(1, 2, PACK)
         load_table(0, 1)
         for i in range(2, GROUPS):
-            for pair in range(PAIRS):
-                load_x(i, pair)
+            load_x(i, 0, PACK)
             if i - 1 < GROUPS_PER_SEQ:
                 for half in range(HALVES):
                     load_table(i - 1, half)
@@ -111,7 +110,7 @@ def tile_linearattention_pa_t_kernel(tc, x, w_k, w_v, cos_tab, sin_tab, out):
         def transpose_x(i, pair):
             bank = flip_psum.tile([P, 2, WORD_BLOCKS, P], F32, name="flip_bank")
             for t in range(2):
-                words = x_rows[(i, pair)][:, t, :].bitcast(F32)
+                words = x_rows[i][:, 2 * pair + t, :].bitcast(F32)
                 for u in range(WORD_BLOCKS):
                     nc.tensor.transpose(bank[:, t, u, :], words[:, u * P : (u + 1) * P], identity[:])
             flipped[(i, pair)] = bank
@@ -215,8 +214,8 @@ def tile_linearattention_pa_t_kernel(tc, x, w_k, w_v, cos_tab, sin_tab, out):
         def rotate(engine, i, h, half, first, last):
             engine.tensor_tensor(
                 out=k_rot[(i, h)][:, half, first:last].rearrange("p (c r) t -> p c t r", r=RUN),
-                in0=k_act[(i, h)][:, :, first:last].rearrange("p t (c r) -> p c t r", r=RUN),
-                in1=tables[i % GROUPS_PER_SEQ][:, half, h, :, first:last].rearrange("p t (c r) -> p c t r", r=RUN),
+                in1=k_act[(i, h)][:, :, first:last].rearrange("p t (c r) -> p c t r", r=RUN),
+                in0=tables[i % GROUPS_PER_SEQ][:, half, h, :, first:last].rearrange("p t (c r) -> p c t r", r=RUN),
                 op=MULT,
             )
 

@@ -24,7 +24,8 @@ INNER = HEADS * HEAD_DIM
 W_COLUMNS = 2 * INNER
 K_ROT_SCALE = 1.0 / 16.0
 RUN = 8
-GPSIMD_COLUMNS = 96
+GPSIMD_COLUMNS = 64
+PASSES_A_STEP = 6
 
 FLOPS = 2 * SEQS * POSITIONS * FEATURES * W_COLUMNS + 2 * SEQS * HEADS * POSITIONS * HALVES * HEAD_DIM * HEAD_DIM
 
@@ -115,11 +116,11 @@ def tile_linearattention_pa_t_kernel(tc, x, w_k, w_v, cos_tab, sin_tab, out):
                     nc.tensor.transpose(bank[:, t, u, :], words[:, u * P : (u + 1) * P], identity[:])
             flipped[(i, pair)] = bank
 
-        def copy_flipped(i, pair):
+        def copy_flipped(i, pair, copy):
             if pair == 0:
                 x_grouped[i] = stream.tile([P, GROUP * PACK], BF16, align_bytes=64, name="x_grouped")
             words = x_grouped[i][:].bitcast(F32).rearrange("q (t m u) -> q t m u", t=PACK, u=WORD_BLOCKS)
-            nc.scalar.copy(
+            copy(
                 out=words[:, 2 * pair : 2 * pair + 2],
                 in_=flipped[(i, pair)][:].rearrange("q t u m -> q t m u"),
             )
@@ -256,24 +257,23 @@ def tile_linearattention_pa_t_kernel(tc, x, w_k, w_v, cos_tab, sin_tab, out):
         open_x_codes(0)
         for pair in range(PAIRS):
             transpose_x(0, pair)
-            copy_flipped(0, pair)
+            copy_flipped(0, pair, nc.scalar.copy)
             quantise_x(0, pair * GROUP // 2, (pair + 1) * GROUP // 2)
         transpose_x(1, 0)
-        copy_flipped(1, 0)
+        copy_flipped(1, 0, nc.scalar.copy)
         project_k_flipped(0)
         project_k(0)
         activate_k_flipped(0)
         activate_k(0)
         transpose_x(1, 1)
-        copy_flipped(1, 1)
-        turn_k(0)
         quantise_weight(raw_v, INNER, "w_v_grouped")
+        copy_flipped(1, 1, nc.vector.tensor_copy)
+        turn_k(0)
         for h in range(HEADS):
             project_v(0, h)
             activate_v(0, h)
         for pair in range(PAIRS):
             transpose_x(2, pair)
-            copy_flipped(2, pair)
 
         def quantise_and_project(i):
             open_x_codes(i)
@@ -283,59 +283,69 @@ def tile_linearattention_pa_t_kernel(tc, x, w_k, w_v, cos_tab, sin_tab, out):
             for h in range(HEADS):
                 project_v(i, h)
 
+        quantise_and_project(1)
+
         blocks = [(h, half) for h in range(HEADS) for half in range(HALVES)]
+        open_blocks, summed = {}, 0
+        first_passes = [(h, half, early) for h, half in blocks for early in range(GROUPS_PER_SEQ)]
         for i in range(GROUPS):
             seq, g = divmod(i, GROUPS_PER_SEQ)
             if g == 0:
                 open_sequence(seq)
             open_k_rot(i)
-            if i + 3 < GROUPS:
+            if 0 < i < GROUPS - 3:
                 for pair in range(PAIRS):
                     transpose_x(i + 3, pair)
             rotate(nc.gpsimd, i, 1, 1, 0, GPSIMD_COLUMNS)
             rotate_on_vector(i)
             if i == 0:
-                quantise_and_project(1)
+                copy_flipped(2, 0, nc.scalar.copy)
             if i + 1 < GROUPS:
                 activate_k_flipped(i + 1)
                 turn_k(i + 1)
+                if i == 0:
+                    copy_flipped(2, 1, nc.scalar.copy)
+                    for pair in range(PAIRS):
+                        transpose_x(3, pair)
                 activate_k(i + 1)
                 for h in range(HEADS):
                     activate_v(i + 1, h)
             if i + 3 < GROUPS:
                 for pair in range(PAIRS):
-                    copy_flipped(i + 3, pair)
-            if i == 0:
-                quantise_v(i)
-            if i + 2 < GROUPS:
-                quantise_and_project(i + 2)
-            if i > 0:
-                quantise_v(i)
-            if i + 1 < GROUPS:
-                for h in range(HEADS):
-                    quantise_k_rot(i, h)
-            if seq == 1 and g < len(blocks):
-                h, half = blocks[g]
+                    copy_flipped(i + 3, pair, nc.scalar.copy)
+            if seq == 1 and first_passes:
                 if g == 0:
                     state_bank = state_psum.tile([P, HEADS, HALVES, HEAD_DIM], F32, name="state_bank")
-                add_up(state_bank[:, h, half, :], 0, h, half, range(GROUPS_PER_SEQ), 0, LAST)
-            if seq == 1 and g == len(blocks):
-                result = seq_pool.tile([P, HEADS, HALVES, HEAD_DIM], F32, name="result")
-                nc.scalar.mul(out=result[:], in_=state_bank[:], mul=K_ROT_SCALE)
-                nc.sync.dma_start(out=out[0].rearrange("h (a j) d -> j h a d", a=HALVES), in_=result[:])
+                for h, half, early in first_passes[:PASSES_A_STEP]:
+                    add_up(state_bank[:, h, half, :], 0, h, half, [early], 0, LAST)
+                first_passes = first_passes[PASSES_A_STEP:]
+            if 0 < i < GROUPS - 2:
+                quantise_and_project(i + 2)
+            if i >= GROUPS - 3:
+                for h, half in blocks[:HALVES]:
+                    if i == GROUPS - 3:
+                        bank = flip_psum.tile([P, PACK, HEAD_DIM], F32, name="flip_bank")
+                        open_blocks[(h, half)] = bank[:, 0, :]
+                    add_up(open_blocks[(h, half)], seq, h, half, range(summed, g - 1 if i + 1 < GROUPS else LAST), 0, LAST)
+                summed = g - 1
+            if i + 1 < GROUPS:
+                quantise_v(i)
+                for h in range(HEADS):
+                    quantise_k_rot(i, h)
+            if i == 0:
+                quantise_and_project(2)
+
+        first_result = seq_pool.tile([P, HEADS, HALVES, HEAD_DIM], F32, name="result")
+        nc.scalar.mul(out=first_result[:], in_=state_bank[:], mul=K_ROT_SCALE)
+        nc.sync.dma_start(out=out[0].rearrange("h (a j) d -> j h a d", a=HALVES), in_=first_result[:])
 
         i, seq = GROUPS - 1, SEQS - 1
-        open_blocks = {}
-        for n, (h, half) in enumerate(blocks):
-            if n == 0:
-                bank = state_psum.tile([P, PACK, HEAD_DIM], F32, name="state_bank")
-            elif n < 3:
-                bank = flip_psum.tile([P, PACK, HEAD_DIM], F32, name="flip_bank")
-            else:
-                bank = k_psum.tile([P, PACK, HEAD_DIM], F32, name="k_bank")
+        for h, half in blocks[HALVES:]:
+            bank = k_psum.tile([P, PACK, HEAD_DIM], F32, name="k_bank" if half else "k_flipped_bank")
             open_blocks[(h, half)] = bank[:, 0, :]
             add_up(open_blocks[(h, half)], seq, h, half, range(LAST), 0, LAST)
         result = seq_pool.tile([P, HEADS, HALVES, HEAD_DIM], F32, name="result")
+        quantise_v(i)
         for h in range(HEADS):
             quantise_k_rot(i, h)
             for half in range(HALVES):

from contextlib import ExitStack

import concourse.mybir as mybir
from concourse.masks import make_identity

F32 = mybir.dt.float32
BF16 = mybir.dt.bfloat16
U32 = mybir.dt.uint32
U8 = mybir.dt.uint8
FP8X4 = mybir.dt.float8_e4m3fn_x4
SILU = mybir.ActivationFunctionType.Silu
MULT = mybir.AluOpType.mult

SEQS, POSITIONS, FEATURES, HEADS, HEAD_DIM = 2, 4096, 512, 2, 128
P = 128
PACK = 4
GROUP = P * PACK
GROUPS_PER_SEQ = POSITIONS // GROUP
GROUPS = SEQS * GROUPS_PER_SEQ
PAIRS = PACK // 2
HALVES = 2
WORD_BLOCKS = FEATURES // 2 // P
INNER = HEADS * HEAD_DIM
W_COLUMNS = 2 * INNER
K_ROT_SCALE = 1.0 / 16.0
RUN = 8
GPSIMD_COLUMNS = 64
PASSES_A_STEP = 6

FLOPS = 2 * SEQS * POSITIONS * FEATURES * W_COLUMNS + 2 * SEQS * HEADS * POSITIONS * HALVES * HEAD_DIM * HEAD_DIM


def tile_linearattention_pa_t_kernel(tc, x, w_k, w_v, cos_tab, sin_tab, out):
    nc = tc.nc
    with ExitStack() as ctx:
        const = ctx.enter_context(tc.tile_pool(name="const", bufs=1))
        x_pool = ctx.enter_context(tc.tile_pool(name="x_rows", bufs=GROUPS))
        table_pool = ctx.enter_context(tc.tile_pool(name="tables", bufs=GROUPS_PER_SEQ))
        seq_pool = ctx.enter_context(tc.tile_pool(name="per_sequence", bufs=SEQS))
        stream = ctx.enter_context(tc.tile_pool(name="stream", bufs=3))
        single = ctx.enter_context(tc.tile_pool(name="single", bufs=1))
        flip_psum = ctx.enter_context(tc.psum_pool(name="flip_psum", bufs=2))
        v_psum = ctx.enter_context(tc.psum_pool(name="v_psum", bufs=2))
        k_psum = ctx.enter_context(tc.psum_pool(name="k_psum", bufs=1))
        state_psum = ctx.enter_context(tc.psum_pool(name="state_psum", bufs=1))
        ctx.enter_context(tc.manual_schedule())

        x_rows, tables = {}, {}

        def load_x(i, first, last):
            seq, g = divmod(i, GROUPS_PER_SEQ)
            positions = x[seq, g * GROUP : (g + 1) * GROUP, :].rearrange("(p t) d -> p t d", t=PACK)
            if first == 0:
                x_rows[i] = x_pool.tile([P, PACK, FEATURES], BF16, name="rows")
            nc.sync.dma_start(out=x_rows[i][:, first:last, :], in_=positions[:, first:last, :])

        def load_weight(w, name):
            raw = const.tile([P, PACK, INNER], BF16, name=name)
            nc.sync.dma_start(
                out=raw[:].rearrange("q (u e) c -> q u (e c)", e=2),
                in_=w.rearrange("(u q e) c -> q u (e c)", u=WORD_BLOCKS, e=2),
            )
            return raw

        def load_table(g, half):
            if half == 0:
                tables[g] = table_pool.tile([P, HALVES, HEADS, PACK, HEAD_DIM], BF16, name="table")
            positions = (cos_tab, sin_tab)[half][:, g * GROUP : (g + 1) * GROUP, :]
            nc.sync.dma_start(out=tables[g][:, half], in_=positions.rearrange("h (p t) w -> p h t w", t=PACK))

        load_x(0, 0, 2)
        raw_k = load_weight(w_k, "raw_k")
        load_x(0, 2, PACK)
        load_x(1, 0, 2)
        raw_v = load_weight(w_v, "raw_v")
        load_table(0, 0)
        load_x(1, 2, PACK)
        load_table(0, 1)
        for i in range(2, GROUPS):
            load_x(i, 0, PACK)
            if i - 1 < GROUPS_PER_SEQ:
                for half in range(HALVES):
                    load_table(i - 1, half)

        identity = const.tile([P, P], F32)
        make_identity(nc, identity[:])
        zero = const.tile([P, 1], F32)
        unused = const.tile([P, 1], F32)
        nc.vector.memset(zero[:], 0.0)
        nc.scalar.activation(out=unused[:], in_=zero[:], func=SILU)

        w_codes = const.tile([P, W_COLUMNS], U32, align_bytes=64)
        w_scales = const.tile([P, W_COLUMNS], U8, align_bytes=64)

        def quantise_weight(raw, first, name):
            grouped = const.tile([P, INNER, PACK], BF16, align_bytes=64, name=name)
            nc.vector.tensor_copy(
                out=grouped[:].rearrange("p (c r) t -> p c t r", r=RUN),
                in_=raw[:].rearrange("p t (c r) -> p c t r", r=RUN),
            )
            nc.vector.quantize_mx(
                out=w_codes[:, first : first + INNER].bitcast(FP8X4),
                scales=w_scales[:, first : first + INNER],
                in_=grouped[:].rearrange("p c t -> p (c t)"),
            )

        flipped, x_grouped, x_codes, x_scales, k_banks, k_flipped_banks, v_banks = {}, {}, {}, {}, {}, {}, {}
        k_flipped, k_act, v_grouped, k_rot = {}, {}, {}, {}
        k_codes, k_scales, v_codes, v_scales = {}, {}, {}, {}

        def transpose_x(i, pair):
            bank = flip_psum.tile([P, 2, WORD_BLOCKS, P], F32, name="flip_bank")
            for t in range(2):
                words = x_rows[i][:, 2 * pair + t, :].bitcast(F32)
                for u in range(WORD_BLOCKS):
                    nc.tensor.transpose(bank[:, t, u, :], words[:, u * P : (u + 1) * P], identity[:])
            flipped[(i, pair)] = bank

        def copy_flipped(i, pair, copy):
            if pair == 0:
                x_grouped[i] = stream.tile([P, GROUP * PACK], BF16, align_bytes=64, name="x_grouped")
            words = x_grouped[i][:].bitcast(F32).rearrange("q (t m u) -> q t m u", t=PACK, u=WORD_BLOCKS)
            copy(
                out=words[:, 2 * pair : 2 * pair + 2],
                in_=flipped[(i, pair)][:].rearrange("q t u m -> q t m u"),
            )

        def open_x_codes(i):
            codes = stream.tile([P, GROUP], U32, align_bytes=64, name="x_codes")
            scales = stream.tile([P, GROUP], U8, align_bytes=64, name="x_scales")
            x_codes[i], x_scales[i] = codes, scales

        def quantise_x(i, first, last):
            nc.vector.quantize_mx(
                out=x_codes[i][:, first:last].bitcast(FP8X4),
                scales=x_scales[i][:, first:last],
                in_=x_grouped[i][:, first * PACK : last * PACK],
            )

        def multiply(bank_columns, i, t, columns):
            rows = slice(t * P, (t + 1) * P)
            nc.tensor.matmul_mx(
                out=bank_columns,
                lhsT=x_codes[i][:, rows].bitcast(FP8X4),
                lhsT_scale=x_scales[i][:, rows],
                rhs=w_codes[:, columns].bitcast(FP8X4),
                rhs_scale=w_scales[:, columns],
                start=True,
                stop=True,
            )

        def project_k_flipped(i):
            bank = k_psum.tile([P, GROUP], F32, name="k_flipped_bank")
            nc.tensor.matmul_mx(
                out=bank[:],
                lhsT=w_codes[:, 0:HEAD_DIM].bitcast(FP8X4),
                lhsT_scale=w_scales[:, 0:HEAD_DIM],
                rhs=x_codes[i][:].bitcast(FP8X4),
                rhs_scale=x_scales[i][:],
                start=True,
                stop=True,
            )
            k_flipped_banks[i] = bank

        def project_k(i):
            bank = k_psum.tile([P, PACK, HEAD_DIM], F32, name="k_bank")
            for t in range(PACK):
                multiply(bank[:, t, :], i, t, slice(HEAD_DIM, INNER))
            k_banks[i] = bank

        def project_v(i, h):
            bank = v_psum.tile([P, PACK, HEAD_DIM], F32, name="v_bank")
            for t in range(PACK):
                multiply(bank[:, t, :], i, t, slice(INNER + h * HEAD_DIM, INNER + (h + 1) * HEAD_DIM))
            v_banks[(i, h)] = bank

        def activate_k_flipped(i):
            k_flipped[i] = stream.tile([P, PACK, P], F32, name="k_flipped")
            nc.scalar.activation(
                out=k_flipped[i][:], in_=k_flipped_banks[i][:].rearrange("j (t p) -> j t p", t=PACK), func=SILU
            )

        def activate_k(i):
            k_act[(i, 1)] = stream.tile([P, PACK, HEAD_DIM], F32, name="k_act")
            nc.scalar.activation(out=k_act[(i, 1)][:], in_=k_banks[i][:], func=SILU)

        def turn_k(i):
            bank = k_psum.tile([P, PACK, HEAD_DIM], F32, name="k_turned")
            for t in range(PACK):
                nc.tensor.transpose(bank[:, t, :], k_flipped[i][:, t, :], identity[:])
            k_act[(i, 0)] = bank

        def activate_v(i, h):
            if h == 0:
                v_grouped[i] = stream.tile([P, HEADS, HEAD_DIM, PACK], BF16, align_bytes=64, name="v_grouped")
            nc.scalar.activation(out=v_grouped[i][:, h], in_=v_banks[(i, h)][:].rearrange("p t w -> p w t"), func=SILU)

        def open_sequence(seq):
            kc = seq_pool.tile([P, GROUPS_PER_SEQ, HALVES * INNER], U32, align_bytes=64, name="k_codes")
            ks = seq_pool.tile([P, GROUPS_PER_SEQ, HALVES * INNER], U8, align_bytes=64, name="k_scales")
            vc = seq_pool.tile([P, GROUPS_PER_SEQ, INNER], U32, align_bytes=64, name="v_codes")
            vs = seq_pool.tile([P, GROUPS_PER_SEQ, INNER], U8, align_bytes=64, name="v_scales")
            k_codes[seq], k_scales[seq], v_codes[seq], v_scales[seq] = kc, ks, vc, vs

        def open_k_rot(i):
            k_rot[(i, 0)] = stream.tile([P, HALVES, HEAD_DIM, PACK], BF16, align_bytes=64, name="k_rot_0")
            k_rot[(i, 1)] = single.tile([P, HALVES, HEAD_DIM, PACK], BF16, align_bytes=64, name="k_rot_1")

        def rotate_on_vector(i):
            rotate(nc.vector, i, 0, 0, 0, HEAD_DIM)
            rotate(nc.vector, i, 0, 1, 0, HEAD_DIM)
            rotate(nc.vector, i, 1, 0, 0, HEAD_DIM)
            rotate(nc.vector, i, 1, 1, GPSIMD_COLUMNS, HEAD_DIM)

        def rotate(engine, i, h, half, first, last):
            engine.tensor_tensor(
                out=k_rot[(i, h)][:, half, first:last].rearrange("p (c r) t -> p c t r", r=RUN),
                in1=k_act[(i, h)][:, :, first:last].rearrange("p t (c r) -> p c t r", r=RUN),
                in0=tables[i % GROUPS_PER_SEQ][:, half, h, :, first:last].rearrange("p t (c r) -> p c t r", r=RUN),
                op=MULT,
            )

        def quantise_v(i):
            seq, g = divmod(i, GROUPS_PER_SEQ)
            nc.vector.quantize_mx(
                out=v_codes[seq][:, g, :].bitcast(FP8X4),
                scales=v_scales[seq][:, g, :],
                in_=v_grouped[i][:].rearrange("p h w t -> p (h w t)"),
            )

        def quantise_k_rot(i, h):
            seq, g = divmod(i, GROUPS_PER_SEQ)
            columns = slice(h * HALVES * HEAD_DIM, (h + 1) * HALVES * HEAD_DIM)
            nc.vector.quantize_mx(
                out=k_codes[seq][:, g, columns].bitcast(FP8X4),
                scales=k_scales[seq][:, g, columns],
                in_=k_rot[(i, h)][:].rearrange("p a c t -> p (a c t)"),
            )

        def add_up(block, seq, h, half, groups, first, last):
            e_columns = slice((h * HALVES + half) * HEAD_DIM, (h * HALVES + half + 1) * HEAD_DIM)
            d_columns = slice(h * HEAD_DIM, (h + 1) * HEAD_DIM)
            for g in groups:
                nc.tensor.matmul_mx(
                    out=block,
                    lhsT=k_codes[seq][:, g, e_columns].bitcast(FP8X4),
                    lhsT_scale=k_scales[seq][:, g, e_columns],
                    rhs=v_codes[seq][:, g, d_columns].bitcast(FP8X4),
                    rhs_scale=v_scales[seq][:, g, d_columns],
                    start=(g == first),
                    stop=(g == last),
                )

        LAST = GROUPS_PER_SEQ - 1

        quantise_weight(raw_k, 0, "k_grouped")
        open_x_codes(0)
        for pair in range(PAIRS):
            transpose_x(0, pair)
            copy_flipped(0, pair, nc.scalar.copy)
            quantise_x(0, pair * GROUP // 2, (pair + 1) * GROUP // 2)
        transpose_x(1, 0)
        copy_flipped(1, 0, nc.scalar.copy)
        project_k_flipped(0)
        project_k(0)
        activate_k_flipped(0)
        activate_k(0)
        transpose_x(1, 1)
        quantise_weight(raw_v, INNER, "w_v_grouped")
        copy_flipped(1, 1, nc.vector.tensor_copy)
        turn_k(0)
        for h in range(HEADS):
            project_v(0, h)
            activate_v(0, h)
        for pair in range(PAIRS):
            transpose_x(2, pair)

        def quantise_and_project(i):
            open_x_codes(i)
            quantise_x(i, 0, GROUP)
            project_k_flipped(i)
            project_k(i)
            for h in range(HEADS):
                project_v(i, h)

        quantise_and_project(1)

        blocks = [(h, half) for h in range(HEADS) for half in range(HALVES)]
        open_blocks, summed = {}, 0
        first_passes = [(h, half, early) for h, half in blocks for early in range(GROUPS_PER_SEQ)]
        for i in range(GROUPS):
            seq, g = divmod(i, GROUPS_PER_SEQ)
            if g == 0:
                open_sequence(seq)
            open_k_rot(i)
            if 0 < i < GROUPS - 3:
                for pair in range(PAIRS):
                    transpose_x(i + 3, pair)
            rotate(nc.gpsimd, i, 1, 1, 0, GPSIMD_COLUMNS)
            rotate_on_vector(i)
            if i == 0:
                copy_flipped(2, 0, nc.scalar.copy)
            if i + 1 < GROUPS:
                activate_k_flipped(i + 1)
                turn_k(i + 1)
                if i == 0:
                    copy_flipped(2, 1, nc.scalar.copy)
                    for pair in range(PAIRS):
                        transpose_x(3, pair)
                activate_k(i + 1)
                for h in range(HEADS):
                    activate_v(i + 1, h)
            if i + 3 < GROUPS:
                for pair in range(PAIRS):
                    copy_flipped(i + 3, pair, nc.scalar.copy)
            if seq == 1 and first_passes:
                if g == 0:
                    state_bank = state_psum.tile([P, HEADS, HALVES, HEAD_DIM], F32, name="state_bank")
                for h, half, early in first_passes[:PASSES_A_STEP]:
                    add_up(state_bank[:, h, half, :], 0, h, half, [early], 0, LAST)
                first_passes = first_passes[PASSES_A_STEP:]
            if 0 < i < GROUPS - 2:
                quantise_and_project(i + 2)
            if i >= GROUPS - 3:
                for h, half in blocks[:HALVES]:
                    if i == GROUPS - 3:
                        bank = flip_psum.tile([P, PACK, HEAD_DIM], F32, name="flip_bank")
                        open_blocks[(h, half)] = bank[:, 0, :]
                    add_up(open_blocks[(h, half)], seq, h, half, range(summed, g - 1 if i + 1 < GROUPS else LAST), 0, LAST)
                summed = g - 1
            if i + 1 < GROUPS:
                quantise_v(i)
                for h in range(HEADS):
                    quantise_k_rot(i, h)
            if i == 0:
                quantise_and_project(2)

        first_result = seq_pool.tile([P, HEADS, HALVES, HEAD_DIM], F32, name="result")
        nc.scalar.mul(out=first_result[:], in_=state_bank[:], mul=K_ROT_SCALE)
        nc.sync.dma_start(out=out[0].rearrange("h (a j) d -> j h a d", a=HALVES), in_=first_result[:])

        i, seq = GROUPS - 1, SEQS - 1
        for h, half in blocks[HALVES:]:
            bank = k_psum.tile([P, PACK, HEAD_DIM], F32, name="k_bank" if half else "k_flipped_bank")
            open_blocks[(h, half)] = bank[:, 0, :]
            add_up(open_blocks[(h, half)], seq, h, half, range(LAST), 0, LAST)
        result = seq_pool.tile([P, HEADS, HALVES, HEAD_DIM], F32, name="result")
        quantise_v(i)
        for h in range(HEADS):
            quantise_k_rot(i, h)
            for half in range(HALVES):
                add_up(open_blocks[(h, half)], seq, h, half, [LAST], 0, LAST)
                nc.scalar.mul(out=result[:, h, half, :], in_=open_blocks[(h, half)], mul=K_ROT_SCALE)
            nc.sync.dma_start(out=out[seq, h].rearrange("(a j) d -> j a d", a=HALVES), in_=result[:, h])
